import numpy as np
import ml_dtypes


def mxq(x, axis, fmt="e4m3"):
    dtype, down = {"e4m3": (ml_dtypes.float8_e4m3fn, 7), "e5m2": (ml_dtypes.float8_e5m2, 14)}[fmt]
    v = np.moveaxis(np.asarray(x, np.float32).astype(ml_dtypes.bfloat16).astype(np.float64), axis, -1)
    blocks = v.reshape(v.shape[:-1] + (-1, 32))
    amax = np.abs(blocks).max(-1, keepdims=True)
    byte = np.maximum(np.where(amax > 0, np.frexp(amax)[1] - 1 + 127, 0) - down, 1)
    scale = np.exp2(byte - 127.0)
    codes = (blocks / scale).astype(np.float32).astype(dtype).astype(np.float64)
    return np.moveaxis((codes * scale).reshape(v.shape), -1, axis)


WIDE = False


def mx_kscale(k):
    if not WIDE:
        return np.ones(k)
    levels = np.array([10, -10, 5, -5, 0])
    a = np.random.permutation(np.resize(levels, k // 512 * 4)).reshape(k // 512, 4)
    idx = np.arange(k)
    return np.exp2(a[idx // 512, idx % 128 // 32])


BF16 = ml_dtypes.bfloat16


def bf(x):
    return np.asarray(x, np.float32).astype(BF16)


def f64(x):
    return np.asarray(x).astype(np.float64)


B, Q, K, D = 4, 256, 256, 512
SIG = 2.0
PMASK = 0.1


def setup_inputs():
    s = mx_kscale(D)
    q = np.random.standard_normal((B, Q, D)) * s
    k = np.random.standard_normal((B, K, D)) * (SIG / np.sqrt(D)) / s
    k[:, :, 0] = np.where(np.random.random((B, K)) < PMASK, 0.0, k[:, :, 0])
    temperature = 1.0 + 0.1 * np.random.standard_normal(1)
    bias = -(np.log(K) + SIG ** 2 / 2.0) + 0.1 * np.random.standard_normal(1)
    return {"queries": bf(q), "keys": bf(k), "temperature": bf(temperature), "bias": bf(bias)}


def reference(queries, keys, temperature, bias):
    kf = f64(keys)
    logits = mxq(f64(queries), 2, "e4m3") @ mxq(kf, 2, "e4m3").transpose(0, 2, 1)
    key_mask = (kf[:, :, 0] == 0.0)[:, None, :]
    logits = np.where(key_mask, -np.inf, logits)
    m = logits.max(-1, keepdims=True)
    e = np.exp(logits - m)
    z = e.sum(-1, keepdims=True)
    approx_max_logit = (np.log(z) + m)[:, :, 0]
    confidence = 1.0 / (1.0 + np.exp(-((approx_max_logit + f64(bias)) * f64(temperature))))
    attn = e / z
    return attn, confidence

@@ -1,0 +1,198 @@
+from contextlib import ExitStack
+
+import concourse.mybir as mybir
+from concourse.masks import make_identity
+
+F32 = mybir.dt.float32
+BF16 = mybir.dt.bfloat16
+U32 = mybir.dt.uint32
+U8 = mybir.dt.uint8
+FP8X4 = mybir.dt.float8_e4m3fn_x4
+ALU = mybir.AluOpType
+ACT = mybir.ActivationFunctionType
+AXIS = mybir.AxisListType
+
+B, Q, K, D = 4, 256, 256, 512
+P = 128
+ROW_TILES = Q // P
+PACK = 4
+WORDS = D // 2
+HALVES = WORDS // P
+BANK = 512
+MASKED = -1.0e30
+
+FLOPS = 2 * B * Q * K * D
+
+
+def tile_contentattention_s_kernel(tc, queries, keys, temperature, bias, out_0, out_1):
+    nc = tc.nc
+    with ExitStack() as ctx:
+        consts = ctx.enter_context(tc.tile_pool(name="consts", bufs=1))
+        per_batch = ctx.enter_context(tc.tile_pool(name="per_batch", bufs=B))
+        psum = ctx.enter_context(tc.psum_pool(name="psum", bufs=2))
+
+        k_rows = []
+        q_rows = []
+        for b in range(B):
+            k_sb = per_batch.tile([P, ROW_TILES * D], BF16)
+            nc.sync.dma_start(
+                out=k_sb[:].rearrange("p (n d) -> p n d", n=ROW_TILES),
+                in_=keys[b].rearrange("(n p) d -> p n d", p=P),
+            )
+            k_rows.append(k_sb)
+            q_sb = per_batch.tile([P, ROW_TILES * D], BF16)
+            nc.sync.dma_start(
+                out=q_sb[:].rearrange("p (n d) -> p n d", n=ROW_TILES),
+                in_=queries[b].rearrange("(n p) d -> p n d", p=P),
+            )
+            q_rows.append(q_sb)
+
+        temp_bf = consts.tile([P, 1], BF16)
+        nc.gpsimd.dma_start(out=temp_bf[:], in_=temperature.partition_broadcast(P))
+        bias_bf = consts.tile([P, 1], BF16)
+        nc.gpsimd.dma_start(out=bias_bf[:], in_=bias.partition_broadcast(P))
+
+        ident = consts.tile([P, P], F32)
+        make_identity(nc, ident[:])
+        conf_cols = consts.tile([P, P], F32)
+        nc.vector.memset(conf_cols[:], 0.0)
+        scratch = consts.tile([P, 1], F32)
+        nc.vector.memset(scratch[:], 0.0)
+        nc.scalar.activation(out=scratch[:], in_=scratch[:], func=ACT.Exp)
+
+        neg_max = consts.tile([P, B * ROW_TILES], F32)
+        row_sum = consts.tile([P, B * ROW_TILES], F32)
+        inv_sum = consts.tile([P, B * ROW_TILES], F32)
+
+        def transpose_words(rows, bank):
+            words = rows[:].bitcast(F32)
+            for piece in range(ROW_TILES * HALVES):
+                cols = slice(piece * P, (piece + 1) * P)
+                nc.tensor.transpose(out=bank[:, cols], in_=words[:, cols], identity=ident[:])
+
+        def regroup(copy, bank, grouped):
+            copy(
+                out=grouped[:].bitcast(F32).rearrange("w (n r h) -> w n r h", n=ROW_TILES, h=HALVES),
+                in_=bank[:].rearrange("w (n h r) -> w n r h", n=ROW_TILES, h=HALVES),
+            )
+
+        operands = {}
+        exps = {}
+
+        def front(b):
+            penalty_col = per_batch.tile([P, ROW_TILES], F32)
+            nc.vector.tensor_scalar(
+                out=penalty_col[:].rearrange("p (n o) -> p n o", o=1),
+                in0=k_rows[b][:].rearrange("p (n d) -> p n d", n=ROW_TILES)[:, :, 0:1],
+                scalar1=0.0,
+                scalar2=MASKED,
+                op0=ALU.is_equal,
+                op1=ALU.mult,
+            )
+
+            k_bank = psum.tile([P, BANK], F32)
+            transpose_words(k_rows[b], k_bank)
+            penalty_bank = psum.tile([P, BANK], F32)
+            for n in range(ROW_TILES):
+                nc.tensor.transpose(
+                    out=penalty_bank[:, n * P : (n + 1) * P],
+                    in_=penalty_col[:, n : n + 1].to_broadcast([P, P]),
+                    identity=ident[:],
+                )
+            q_bank = psum.tile([P, BANK], F32)
+            transpose_words(q_rows[b], q_bank)
+
+            k_grouped = per_batch.tile([P, K * PACK], BF16, align_bytes=64)
+            regroup(nc.scalar.copy, k_bank, k_grouped)
+            q_grouped = per_batch.tile([P, Q * PACK], BF16, align_bytes=64)
+            regroup(nc.scalar.copy, q_bank, q_grouped)
+            penalty = per_batch.tile([P, K], F32)
+            nc.scalar.copy(out=penalty[:], in_=penalty_bank[:, 0:K])
+
+            k_codes = per_batch.tile([P, K], U32, align_bytes=64)
+            k_scales = per_batch.tile([P, K], U8, align_bytes=64)
+            nc.vector.quantize_mx(out=k_codes[:].bitcast(FP8X4), scales=k_scales[:], in_=k_grouped[:])
+            q_codes = per_batch.tile([P, Q], U32, align_bytes=64)
+            q_scales = per_batch.tile([P, Q], U8, align_bytes=64)
+            nc.vector.quantize_mx(out=q_codes[:].bitcast(FP8X4), scales=q_scales[:], in_=q_grouped[:])
+            operands[b] = (k_codes, k_scales, q_codes, q_scales, penalty)
+
+        def middle(b):
+            k_codes, k_scales, q_codes, q_scales, penalty = operands[b]
+            logits = psum.tile([P, ROW_TILES * K], F32)
+            for n in range(ROW_TILES):
+                q_cols = slice(n * P, (n + 1) * P)
+                nc.tensor.matmul_mx(
+                    out=logits[:, n * K : (n + 1) * K],
+                    lhsT=q_codes[:, q_cols].bitcast(FP8X4),
+                    lhsT_scale=q_scales[:, q_cols],
+                    rhs=k_codes[:].bitcast(FP8X4),
+                    rhs_scale=k_scales[:],
+                    start=True,
+                    stop=True,
+                )
+            masked = per_batch.tile([P, ROW_TILES, K], F32)
+            nc.vector.tensor_tensor(
+                out=masked[:],
+                in0=logits[:].rearrange("p (n k) -> p n k", n=ROW_TILES),
+                in1=penalty[:].unsqueeze(1).to_broadcast([P, ROW_TILES, K]),
+                op=ALU.add,
+            )
+            stat_cols = slice(b * ROW_TILES, (b + 1) * ROW_TILES)
+            nc.vector.tensor_reduce(
+                out=neg_max[:, stat_cols], in_=masked[:], axis=AXIS.X, op=ALU.max, negate=True
+            )
+            expd = per_batch.tile([P, ROW_TILES, K], F32)
+            for n in range(ROW_TILES):
+                col = b * ROW_TILES + n
+                nc.scalar.activation(
+                    out=expd[:, n, :],
+                    in_=masked[:, n, :],
+                    func=ACT.Exp,
+                    bias=neg_max[:, col : col + 1],
+                    accum_out=row_sum[:, col : col + 1],
+                )
+            exps[b] = expd
+
+        def back(b):
+            expd = exps[b]
+            stat_cols = slice(b * ROW_TILES, (b + 1) * ROW_TILES)
+            nc.vector.reciprocal(out=inv_sum[:, stat_cols], in_=row_sum[:, stat_cols])
+            attn = per_batch.tile([P, ROW_TILES, K], F32)
+            for n in range(ROW_TILES):
+                col = b * ROW_TILES + n
+                nc.vector.tensor_scalar_mul(
+                    out=attn[:, n, :], in0=expd[:, n, :], scalar1=inv_sum[:, col : col + 1]
+                )
+            nc.sync.dma_start(out=out_0[b].rearrange("(n p) k -> p n k", p=P), in_=attn[:])
+
+        for step in range(B + 2):
+            if step < B:
+                front(step)
+            if 0 <= step - 1 < B:
+                middle(step - 1)
+            if 0 <= step - 2 < B:
+                back(step - 2)
+
+        temp = consts.tile([P, 1], F32)
+        nc.vector.tensor_copy(out=temp[:], in_=temp_bf[:])
+        bias_temp = consts.tile([P, 1], F32)
+        nc.vector.tensor_tensor(out=bias_temp[:], in0=bias_bf[:], in1=temp_bf[:], op=ALU.mult)
+        log_sum = consts.tile([P, B * ROW_TILES], F32)
+        nc.scalar.activation(out=log_sum[:], in_=row_sum[:], func=ACT.Ln)
+        lse = consts.tile([P, B * ROW_TILES], F32)
+        nc.vector.tensor_tensor(out=lse[:], in0=log_sum[:], in1=neg_max[:], op=ALU.subtract)
+        nc.scalar.activation(
+            out=conf_cols[:, 0 : B * ROW_TILES],
+            in_=lse[:],
+            func=ACT.Sigmoid,
+            scale=temp[:],
+            bias=bias_temp[:],
+        )
+        conf_bank = psum.tile([P, BANK], F32, tag="penalty_bank")
+        nc.tensor.transpose(out=conf_bank[:, 0:P], in_=conf_cols[:], identity=ident[:])
+        conf_rows = consts.tile([P, P], F32)
+        nc.scalar.copy(out=conf_rows[:], in_=conf_bank[:, 0:P])
+        nc.sync.dma_start(
+            out=out_1.rearrange("b (n p) -> (b n) p", p=P), in_=conf_rows[0 : B * ROW_TILES, :]
+        )

@@ -19,7 +19,9 @@ PACK = 4
 WORDS = D // 2
 HALVES = WORDS // P
 BANK = 512
-MASKED = -1.0e30
+STATS = B * ROW_TILES
+AHEAD = 2
+MASKED = -(2.0**100)
 
 FLOPS = 2 * B * Q * K * D
 
@@ -27,18 +29,21 @@ FLOPS = 2 * B * Q * K * D
 def tile_contentattention_s_kernel(tc, queries, keys, temperature, bias, out_0, out_1):
     nc = tc.nc
     with ExitStack() as ctx:
+        ctx.enter_context(tc.manual_schedule())
         consts = ctx.enter_context(tc.tile_pool(name="consts", bufs=1))
         per_batch = ctx.enter_context(tc.tile_pool(name="per_batch", bufs=B))
         psum = ctx.enter_context(tc.psum_pool(name="psum", bufs=2))
+
+        temp_bf = consts.tile([P, 1], BF16)
+        nc.scalar.dma_start(out=temp_bf[:], in_=temperature.partition_broadcast(P))
+        bias_bf = consts.tile([P, 1], BF16)
+        nc.scalar.dma_start(out=bias_bf[:], in_=bias.partition_broadcast(P))
 
         k_rows = []
         q_rows = []
         for b in range(B):
             k_sb = per_batch.tile([P, ROW_TILES * D], BF16)
-            nc.sync.dma_start(
-                out=k_sb[:].rearrange("p (n d) -> p n d", n=ROW_TILES),
-                in_=keys[b].rearrange("(n p) d -> p n d", p=P),
-            )
+            nc.sync.dma_start(out=k_sb[:], in_=keys[b].rearrange("(p n) d -> p (n d)", n=ROW_TILES))
             k_rows.append(k_sb)
             q_sb = per_batch.tile([P, ROW_TILES * D], BF16)
             nc.sync.dma_start(
@@ -47,41 +52,33 @@ def tile_contentattention_s_kernel(tc, queries, keys, temperature, bias, out_0, 
             )
             q_rows.append(q_sb)
 
-        temp_bf = consts.tile([P, 1], BF16)
-        nc.gpsimd.dma_start(out=temp_bf[:], in_=temperature.partition_broadcast(P))
-        bias_bf = consts.tile([P, 1], BF16)
-        nc.gpsimd.dma_start(out=bias_bf[:], in_=bias.partition_broadcast(P))
-
         ident = consts.tile([P, P], F32)
-        make_identity(nc, ident[:])
+        nc.vector.memset(ident[:], 0.0)
+        make_identity(nc, ident[:], nomemset=True)
         conf_cols = consts.tile([P, P], F32)
         nc.vector.memset(conf_cols[:], 0.0)
         scratch = consts.tile([P, 1], F32)
         nc.vector.memset(scratch[:], 0.0)
         nc.scalar.activation(out=scratch[:], in_=scratch[:], func=ACT.Exp)
 
-        neg_max = consts.tile([P, B * ROW_TILES], F32)
-        row_sum = consts.tile([P, B * ROW_TILES], F32)
-        inv_sum = consts.tile([P, B * ROW_TILES], F32)
+        temp = consts.tile([P, 1], F32)
+        nc.vector.tensor_copy(out=temp[:], in_=temp_bf[:])
+        neg_temp = consts.tile([P, 1], F32)
+        nc.vector.tensor_scalar_mul(out=neg_temp[:], in0=temp_bf[:], scalar1=-1.0)
+        neg_bias_temp = consts.tile([P, 1], F32)
+        nc.vector.scalar_tensor_tensor(
+            out=neg_bias_temp[:], in0=bias_bf[:], scalar=-1.0, in1=temp_bf[:], op0=ALU.mult, op1=ALU.mult
+        )
 
-        def transpose_words(rows, bank):
-            words = rows[:].bitcast(F32)
-            for piece in range(ROW_TILES * HALVES):
-                cols = slice(piece * P, (piece + 1) * P)
-                nc.tensor.transpose(out=bank[:, cols], in_=words[:, cols], identity=ident[:])
+        neg_max = consts.tile([P, STATS], F32)
+        row_sum = consts.tile([P, STATS], F32)
+        inv_sum = consts.tile([P, STATS], F32)
+        sum_pow = consts.tile([P, STATS], F32)
 
-        def regroup(copy, bank, grouped):
-            copy(
-                out=grouped[:].bitcast(F32).rearrange("w (n r h) -> w n r h", n=ROW_TILES, h=HALVES),
-                in_=bank[:].rearrange("w (n h r) -> w n r h", n=ROW_TILES, h=HALVES),
-            )
-
-        operands = {}
-        exps = {}
-
-        def front(b):
-            penalty_col = per_batch.tile([P, ROW_TILES], F32)
-            nc.vector.tensor_scalar(
+        penalty_cols = []
+        for b in range(B):
+            penalty_col = per_batch.tile([P, ROW_TILES], BF16)
+            nc.gpsimd.tensor_scalar(
                 out=penalty_col[:].rearrange("p (n o) -> p n o", o=1),
                 in0=k_rows[b][:].rearrange("p (n d) -> p n d", n=ROW_TILES)[:, :, 0:1],
                 scalar1=0.0,
@@ -89,25 +86,41 @@ def tile_contentattention_s_kernel(tc, queries, keys, temperature, bias, out_0, 
                 op0=ALU.is_equal,
                 op1=ALU.mult,
             )
+            penalty_cols.append(penalty_col)
 
+        def transpose_words(rows, bank):
+            words = rows[:].bitcast(F32)
+            for piece in range(ROW_TILES * HALVES):
+                cols = slice(piece * P, (piece + 1) * P)
+                nc.tensor.transpose(out=bank[:, cols], in_=words[:, cols], identity=ident[:])
+
+        operands = {}
+        exps = {}
+
+        def prepare(b, copy_keys):
             k_bank = psum.tile([P, BANK], F32)
             transpose_words(k_rows[b], k_bank)
             penalty_bank = psum.tile([P, BANK], F32)
-            for n in range(ROW_TILES):
-                nc.tensor.transpose(
-                    out=penalty_bank[:, n * P : (n + 1) * P],
-                    in_=penalty_col[:, n : n + 1].to_broadcast([P, P]),
-                    identity=ident[:],
-                )
+            nc.tensor.transpose(
+                out=penalty_bank[:, 0:P],
+                in_=penalty_cols[b][:].bitcast(F32).to_broadcast([P, P]),
+                identity=ident[:],
+            )
             q_bank = psum.tile([P, BANK], F32)
             transpose_words(q_rows[b], q_bank)
 
             k_grouped = per_batch.tile([P, K * PACK], BF16, align_bytes=64)
-            regroup(nc.scalar.copy, k_bank, k_grouped)
+            copy_keys(
+                out=k_grouped[:].bitcast(F32).rearrange("w (p n h) -> w p n h", n=ROW_TILES, h=HALVES),
+                in_=k_bank[:].rearrange("w (n h p) -> w p n h", n=ROW_TILES, h=HALVES),
+            )
+            penalty = per_batch.tile([P, K], BF16)
+            nc.scalar.copy(out=penalty[:].bitcast(F32), in_=penalty_bank[:, 0:P])
             q_grouped = per_batch.tile([P, Q * PACK], BF16, align_bytes=64)
-            regroup(nc.scalar.copy, q_bank, q_grouped)
-            penalty = per_batch.tile([P, K], F32)
-            nc.scalar.copy(out=penalty[:], in_=penalty_bank[:, 0:K])
+            nc.scalar.copy(
+                out=q_grouped[:].bitcast(F32).rearrange("w (n p h) -> w n p h", n=ROW_TILES, h=HALVES),
+                in_=q_bank[:].rearrange("w (n h p) -> w n p h", n=ROW_TILES, h=HALVES),
+            )
 
             k_codes = per_batch.tile([P, K], U32, align_bytes=64)
             k_scales = per_batch.tile([P, K], U8, align_bytes=64)
@@ -117,7 +130,7 @@ def tile_contentattention_s_kernel(tc, queries, keys, temperature, bias, out_0, 
             nc.vector.quantize_mx(out=q_codes[:].bitcast(FP8X4), scales=q_scales[:], in_=q_grouped[:])
             operands[b] = (k_codes, k_scales, q_codes, q_scales, penalty)
 
-        def middle(b):
+        def masked_logits(b):
             k_codes, k_scales, q_codes, q_scales, penalty = operands[b]
             logits = psum.tile([P, ROW_TILES * K], F32)
             for n in range(ROW_TILES):
@@ -142,6 +155,9 @@ def tile_contentattention_s_kernel(tc, queries, keys, temperature, bias, out_0, 
             nc.vector.tensor_reduce(
                 out=neg_max[:, stat_cols], in_=masked[:], axis=AXIS.X, op=ALU.max, negate=True
             )
+            return masked
+
+        def exponentials(b, masked):
             expd = per_batch.tile([P, ROW_TILES, K], F32)
             for n in range(ROW_TILES):
                 col = b * ROW_TILES + n
@@ -154,45 +170,52 @@ def tile_contentattention_s_kernel(tc, queries, keys, temperature, bias, out_0, 
                 )
             exps[b] = expd
 
-        def back(b):
+        def normalise(b):
             expd = exps[b]
-            stat_cols = slice(b * ROW_TILES, (b + 1) * ROW_TILES)
+            first = b * ROW_TILES
+            stat_cols = slice(first, first + ROW_TILES)
+            nc.gpsimd.tensor_tensor(
+                out=sum_pow[:, stat_cols],
+                in0=row_sum[:, stat_cols],
+                in1=neg_temp[:].to_broadcast([P, ROW_TILES]),
+                op=ALU.pow,
+            )
             nc.vector.reciprocal(out=inv_sum[:, stat_cols], in_=row_sum[:, stat_cols])
             attn = per_batch.tile([P, ROW_TILES, K], F32)
-            for n in range(ROW_TILES):
-                col = b * ROW_TILES + n
-                nc.vector.tensor_scalar_mul(
-                    out=attn[:, n, :], in0=expd[:, n, :], scalar1=inv_sum[:, col : col + 1]
-                )
+            nc.gpsimd.tensor_scalar(
+                out=attn[:, 0, :],
+                in0=expd[:, 0, :],
+                scalar1=inv_sum[:, first : first + 1],
+                scalar2=0.0,
+                op0=ALU.mult,
+                op1=ALU.add,
+            )
+            nc.vector.tensor_scalar_mul(
+                out=attn[:, 1, :], in0=expd[:, 1, :], scalar1=inv_sum[:, first + 1 : first + 2]
+            )
             nc.sync.dma_start(out=out_0[b].rearrange("(n p) k -> p n k", p=P), in_=attn[:])
 
-        for step in range(B + 2):
-            if step < B:
-                front(step)
-            if 0 <= step - 1 < B:
-                middle(step - 1)
-            if 0 <= step - 2 < B:
-                back(step - 2)
+        for b in range(AHEAD):
+            prepare(b, nc.vector.tensor_copy)
+        for b in range(B):
+            masked = masked_logits(b)
+            if b >= 1:
+                normalise(b - 1)
+            if b + AHEAD < B:
+                prepare(b + AHEAD, nc.scalar.copy)
+            exponentials(b, masked)
+        normalise(B - 1)
 
-        temp = consts.tile([P, 1], F32)
-        nc.vector.tensor_copy(out=temp[:], in_=temp_bf[:])
-        bias_temp = consts.tile([P, 1], F32)
-        nc.vector.tensor_tensor(out=bias_temp[:], in0=bias_bf[:], in1=temp_bf[:], op=ALU.mult)
-        log_sum = consts.tile([P, B * ROW_TILES], F32)
-        nc.scalar.activation(out=log_sum[:], in_=row_sum[:], func=ACT.Ln)
-        lse = consts.tile([P, B * ROW_TILES], F32)
-        nc.vector.tensor_tensor(out=lse[:], in0=log_sum[:], in1=neg_max[:], op=ALU.subtract)
+        exp_part = consts.tile([P, STATS], F32)
         nc.scalar.activation(
-            out=conf_cols[:, 0 : B * ROW_TILES],
-            in_=lse[:],
-            func=ACT.Sigmoid,
-            scale=temp[:],
-            bias=bias_temp[:],
+            out=exp_part[:], in_=neg_max[:], func=ACT.Exp, scale=temp[:], bias=neg_bias_temp[:]
         )
+        denom = consts.tile([P, STATS], F32)
+        nc.vector.tensor_tensor(out=denom[:], in0=sum_pow[:], in1=exp_part[:], op=ALU.mult)
+        nc.vector.tensor_scalar_add(out=denom[:], in0=denom[:], scalar1=1.0)
+        nc.vector.reciprocal(out=conf_cols[:, 0:STATS], in_=denom[:])
         conf_bank = psum.tile([P, BANK], F32, tag="penalty_bank")
         nc.tensor.transpose(out=conf_bank[:, 0:P], in_=conf_cols[:], identity=ident[:])
         conf_rows = consts.tile([P, P], F32)
         nc.scalar.copy(out=conf_rows[:], in_=conf_bank[:, 0:P])
-        nc.sync.dma_start(
-            out=out_1.rearrange("b (n p) -> (b n) p", p=P), in_=conf_rows[0 : B * ROW_TILES, :]
-        )
+        nc.sync.dma_start(out=out_1.rearrange("b (n p) -> (b n) p", p=P), in_=conf_rows[0:STATS, :])

@@ -151,10 +151,11 @@ def tile_contentattention_s_kernel(tc, queries, keys, temperature, bias, out_0, 
                 in1=penalty[:].unsqueeze(1).to_broadcast([P, ROW_TILES, K]),
                 op=ALU.add,
             )
-            stat_cols = slice(b * ROW_TILES, (b + 1) * ROW_TILES)
-            nc.vector.tensor_reduce(
-                out=neg_max[:, stat_cols], in_=masked[:], axis=AXIS.X, op=ALU.max, negate=True
-            )
+            for n in range(ROW_TILES):
+                col = b * ROW_TILES + n
+                nc.vector.tensor_reduce(
+                    out=neg_max[:, col : col + 1], in_=masked[:, n, :], axis=AXIS.X, op=ALU.max, negate=True
+                )
             return masked
 
         def exponentials(b, masked):
@@ -182,28 +183,24 @@ def tile_contentattention_s_kernel(tc, queries, keys, temperature, bias, out_0, 
             )
             nc.vector.reciprocal(out=inv_sum[:, stat_cols], in_=row_sum[:, stat_cols])
             attn = per_batch.tile([P, ROW_TILES, K], F32)
-            nc.gpsimd.tensor_scalar(
-                out=attn[:, 0, :],
-                in0=expd[:, 0, :],
-                scalar1=inv_sum[:, first : first + 1],
-                scalar2=0.0,
-                op0=ALU.mult,
-                op1=ALU.add,
-            )
-            nc.vector.tensor_scalar_mul(
-                out=attn[:, 1, :], in0=expd[:, 1, :], scalar1=inv_sum[:, first + 1 : first + 2]
-            )
+            for n in range(ROW_TILES):
+                nc.scalar.activation(
+                    out=attn[:, n, :],
+                    in_=expd[:, n, :],
+                    func=ACT.Copy,
+                    scale=inv_sum[:, first + n : first + n + 1],
+                )
             nc.sync.dma_start(out=out_0[b].rearrange("(n p) k -> p n k", p=P), in_=attn[:])
 
         for b in range(AHEAD):
             prepare(b, nc.vector.tensor_copy)
         for b in range(B):
             masked = masked_logits(b)
-            if b >= 1:
-                normalise(b - 1)
             if b + AHEAD < B:
                 prepare(b + AHEAD, nc.scalar.copy)
             exponentials(b, masked)
+            if b >= 1:
+                normalise(b - 1)
         normalise(B - 1)
 
         exp_part = consts.tile([P, STATS], F32)
@@ -217,5 +214,5 @@ def tile_contentattention_s_kernel(tc, queries, keys, temperature, bias, out_0, 
         conf_bank = psum.tile([P, BANK], F32, tag="penalty_bank")
         nc.tensor.transpose(out=conf_bank[:, 0:P], in_=conf_cols[:], identity=ident[:])
         conf_rows = consts.tile([P, P], F32)
-        nc.scalar.copy(out=conf_rows[:], in_=conf_bank[:, 0:P])
+        nc.vector.tensor_copy(out=conf_rows[:], in_=conf_bank[:, 0:P])
         nc.sync.dma_start(out=out_1.rearrange("b (n p) -> (b n) p", p=P), in_=conf_rows[0:STATS, :])

@@ -63,8 +63,6 @@ def tile_contentattention_s_kernel(tc, queries, keys, temperature, bias, out_0, 
 
         temp = consts.tile([P, 1], F32)
         nc.vector.tensor_copy(out=temp[:], in_=temp_bf[:])
-        neg_temp = consts.tile([P, 1], F32)
-        nc.vector.tensor_scalar_mul(out=neg_temp[:], in0=temp_bf[:], scalar1=-1.0)
         neg_bias_temp = consts.tile([P, 1], F32)
         nc.vector.scalar_tensor_tensor(
             out=neg_bias_temp[:], in0=bias_bf[:], scalar=-1.0, in1=temp_bf[:], op0=ALU.mult, op1=ALU.mult
@@ -74,6 +72,7 @@ def tile_contentattention_s_kernel(tc, queries, keys, temperature, bias, out_0, 
         row_sum = consts.tile([P, STATS], F32)
         inv_sum = consts.tile([P, STATS], F32)
         sum_pow = consts.tile([P, STATS], F32)
+        exp_part = consts.tile([P, STATS], F32)
 
         penalty_cols = []
         for b in range(B):
@@ -100,27 +99,27 @@ def tile_contentattention_s_kernel(tc, queries, keys, temperature, bias, out_0, 
         def prepare(b, copy_keys):
             k_bank = psum.tile([P, BANK], F32)
             transpose_words(k_rows[b], k_bank)
+            q_bank = psum.tile([P, BANK], F32)
+            transpose_words(q_rows[b], q_bank)
             penalty_bank = psum.tile([P, BANK], F32)
             nc.tensor.transpose(
                 out=penalty_bank[:, 0:P],
                 in_=penalty_cols[b][:].bitcast(F32).to_broadcast([P, P]),
                 identity=ident[:],
             )
-            q_bank = psum.tile([P, BANK], F32)
-            transpose_words(q_rows[b], q_bank)
 
             k_grouped = per_batch.tile([P, K * PACK], BF16, align_bytes=64)
             copy_keys(
                 out=k_grouped[:].bitcast(F32).rearrange("w (p n h) -> w p n h", n=ROW_TILES, h=HALVES),
                 in_=k_bank[:].rearrange("w (n h p) -> w p n h", n=ROW_TILES, h=HALVES),
             )
-            penalty = per_batch.tile([P, K], BF16)
-            nc.scalar.copy(out=penalty[:].bitcast(F32), in_=penalty_bank[:, 0:P])
             q_grouped = per_batch.tile([P, Q * PACK], BF16, align_bytes=64)
             nc.scalar.copy(
                 out=q_grouped[:].bitcast(F32).rearrange("w (n p h) -> w n p h", n=ROW_TILES, h=HALVES),
                 in_=q_bank[:].rearrange("w (n h p) -> w n p h", n=ROW_TILES, h=HALVES),
             )
+            penalty = per_batch.tile([P, K], BF16)
+            nc.scalar.copy(out=penalty[:].bitcast(F32), in_=penalty_bank[:, 0:P])
 
             k_codes = per_batch.tile([P, K], U32, align_bytes=64)
             k_scales = per_batch.tile([P, K], U8, align_bytes=64)
@@ -169,19 +168,27 @@ def tile_contentattention_s_kernel(tc, queries, keys, temperature, bias, out_0, 
                     bias=neg_max[:, col : col + 1],
                     accum_out=row_sum[:, col : col + 1],
                 )
+            stat_cols = slice(b * ROW_TILES, (b + 1) * ROW_TILES)
+            nc.scalar.activation(
+                out=exp_part[:, stat_cols],
+                in_=neg_max[:, stat_cols],
+                func=ACT.Exp,
+                scale=temp[:],
+                bias=neg_bias_temp[:],
+            )
             exps[b] = expd
 
         def normalise(b):
             expd = exps[b]
             first = b * ROW_TILES
             stat_cols = slice(first, first + ROW_TILES)
+            nc.vector.reciprocal(out=inv_sum[:, stat_cols], in_=row_sum[:, stat_cols])
             nc.gpsimd.tensor_tensor(
                 out=sum_pow[:, stat_cols],
-                in0=row_sum[:, stat_cols],
-                in1=neg_temp[:].to_broadcast([P, ROW_TILES]),
+                in0=inv_sum[:, stat_cols],
+                in1=temp[:].to_broadcast([P, ROW_TILES]),
                 op=ALU.pow,
             )
-            nc.vector.reciprocal(out=inv_sum[:, stat_cols], in_=row_sum[:, stat_cols])
             attn = per_batch.tile([P, ROW_TILES, K], F32)
             for n in range(ROW_TILES):
                 nc.scalar.activation(
@@ -190,7 +197,7 @@ def tile_contentattention_s_kernel(tc, queries, keys, temperature, bias, out_0, 
                     func=ACT.Copy,
                     scale=inv_sum[:, first + n : first + n + 1],
                 )
-            nc.sync.dma_start(out=out_0[b].rearrange("(n p) k -> p n k", p=P), in_=attn[:])
+                nc.sync.dma_start(out=out_0[b, n * P : (n + 1) * P, :], in_=attn[:, n, :])
 
         for b in range(AHEAD):
             prepare(b, nc.vector.tensor_copy)
@@ -203,10 +210,6 @@ def tile_contentattention_s_kernel(tc, queries, keys, temperature, bias, out_0, 
                 normalise(b - 1)
         normalise(B - 1)
 
-        exp_part = consts.tile([P, STATS], F32)
-        nc.scalar.activation(
-            out=exp_part[:], in_=neg_max[:], func=ACT.Exp, scale=temp[:], bias=neg_bias_temp[:]
-        )
         denom = consts.tile([P, STATS], F32)
         nc.vector.tensor_tensor(out=denom[:], in0=sum_pow[:], in1=exp_part[:], op=ALU.mult)
         nc.vector.tensor_scalar_add(out=denom[:], in0=denom[:], scalar1=1.0)

@@ -43,13 +43,14 @@ def tile_contentattention_s_kernel(tc, queries, keys, temperature, bias, out_0, 
         q_rows = []
         for b in range(B):
             k_sb = per_batch.tile([P, ROW_TILES * D], BF16)
-            nc.sync.dma_start(out=k_sb[:], in_=keys[b].rearrange("(p n) d -> p (n d)", n=ROW_TILES))
-            k_rows.append(k_sb)
             q_sb = per_batch.tile([P, ROW_TILES * D], BF16)
-            nc.sync.dma_start(
-                out=q_sb[:].rearrange("p (n d) -> p n d", n=ROW_TILES),
-                in_=queries[b].rearrange("(n p) d -> p n d", p=P),
-            )
+            k_tiles = keys[b].rearrange("(p n) d -> p n d", n=ROW_TILES)
+            q_tiles = queries[b].rearrange("(n p) d -> p n d", p=P)
+            for n in range(ROW_TILES):
+                nc.sync.dma_start(out=k_sb[:, n * D : (n + 1) * D], in_=k_tiles[:, n, :])
+            for n in range(ROW_TILES):
+                nc.sync.dma_start(out=q_sb[:, n * D : (n + 1) * D], in_=q_tiles[:, n, :])
+            k_rows.append(k_sb)
             q_rows.append(q_sb)
 
         ident = consts.tile([P, P], F32)
@@ -63,6 +64,8 @@ def tile_contentattention_s_kernel(tc, queries, keys, temperature, bias, out_0, 
 
         temp = consts.tile([P, 1], F32)
         nc.vector.tensor_copy(out=temp[:], in_=temp_bf[:])
+        neg_temp = consts.tile([P, 1], F32)
+        nc.vector.tensor_scalar_mul(out=neg_temp[:], in0=temp_bf[:], scalar1=-1.0)
         neg_bias_temp = consts.tile([P, 1], F32)
         nc.vector.scalar_tensor_tensor(
             out=neg_bias_temp[:], in0=bias_bf[:], scalar=-1.0, in1=temp_bf[:], op0=ALU.mult, op1=ALU.mult
@@ -169,6 +172,12 @@ def tile_contentattention_s_kernel(tc, queries, keys, temperature, bias, out_0, 
                     accum_out=row_sum[:, col : col + 1],
                 )
             stat_cols = slice(b * ROW_TILES, (b + 1) * ROW_TILES)
+            nc.gpsimd.tensor_tensor(
+                out=sum_pow[:, stat_cols],
+                in0=row_sum[:, stat_cols],
+                in1=neg_temp[:].to_broadcast([P, ROW_TILES]),
+                op=ALU.pow,
+            )
             nc.scalar.activation(
                 out=exp_part[:, stat_cols],
                 in_=neg_max[:, stat_cols],
@@ -183,12 +192,6 @@ def tile_contentattention_s_kernel(tc, queries, keys, temperature, bias, out_0, 
             first = b * ROW_TILES
             stat_cols = slice(first, first + ROW_TILES)
             nc.vector.reciprocal(out=inv_sum[:, stat_cols], in_=row_sum[:, stat_cols])
-            nc.gpsimd.tensor_tensor(
-                out=sum_pow[:, stat_cols],
-                in0=inv_sum[:, stat_cols],
-                in1=temp[:].to_broadcast([P, ROW_TILES]),
-                op=ALU.pow,
-            )
             attn = per_batch.tile([P, ROW_TILES, K], F32)
             for n in range(ROW_TILES):
                 nc.scalar.activation(

from contextlib import ExitStack

import concourse.mybir as mybir
from concourse.masks import make_identity

F32 = mybir.dt.float32
BF16 = mybir.dt.bfloat16
U32 = mybir.dt.uint32
U8 = mybir.dt.uint8
FP8X4 = mybir.dt.float8_e4m3fn_x4
ALU = mybir.AluOpType
ACT = mybir.ActivationFunctionType
AXIS = mybir.AxisListType

B, Q, K, D = 4, 256, 256, 512
P = 128
ROW_TILES = Q // P
PACK = 4
WORDS = D // 2
HALVES = WORDS // P
BANK = 512
STATS = B * ROW_TILES
AHEAD = 2
MASKED = -(2.0**100)

FLOPS = 2 * B * Q * K * D


def tile_contentattention_s_kernel(tc, queries, keys, temperature, bias, out_0, out_1):
    nc = tc.nc
    with ExitStack() as ctx:
        ctx.enter_context(tc.manual_schedule())
        consts = ctx.enter_context(tc.tile_pool(name="consts", bufs=1))
        per_batch = ctx.enter_context(tc.tile_pool(name="per_batch", bufs=B))
        psum = ctx.enter_context(tc.psum_pool(name="psum", bufs=2))

        temp_bf = consts.tile([P, 1], BF16)
        nc.scalar.dma_start(out=temp_bf[:], in_=temperature.partition_broadcast(P))
        bias_bf = consts.tile([P, 1], BF16)
        nc.scalar.dma_start(out=bias_bf[:], in_=bias.partition_broadcast(P))

        k_rows = []
        q_rows = []
        for b in range(B):
            k_sb = per_batch.tile([P, ROW_TILES * D], BF16)
            q_sb = per_batch.tile([P, ROW_TILES * D], BF16)
            k_tiles = keys[b].rearrange("(p n) d -> p n d", n=ROW_TILES)
            q_tiles = queries[b].rearrange("(n p) d -> p n d", p=P)
            for n in range(ROW_TILES):
                nc.sync.dma_start(out=k_sb[:, n * D : (n + 1) * D], in_=k_tiles[:, n, :])
            for n in range(ROW_TILES):
                nc.sync.dma_start(out=q_sb[:, n * D : (n + 1) * D], in_=q_tiles[:, n, :])
            k_rows.append(k_sb)
            q_rows.append(q_sb)

        ident = consts.tile([P, P], F32)
        nc.vector.memset(ident[:], 0.0)
        make_identity(nc, ident[:], nomemset=True)
        conf_cols = consts.tile([P, P], F32)
        nc.vector.memset(conf_cols[:], 0.0)
        scratch = consts.tile([P, 1], F32)
        nc.vector.memset(scratch[:], 0.0)
        nc.scalar.activation(out=scratch[:], in_=scratch[:], func=ACT.Exp)

        temp = consts.tile([P, 1], F32)
        nc.vector.tensor_copy(out=temp[:], in_=temp_bf[:])
        neg_temp = consts.tile([P, 1], F32)
        nc.vector.tensor_scalar_mul(out=neg_temp[:], in0=temp_bf[:], scalar1=-1.0)
        neg_bias_temp = consts.tile([P, 1], F32)
        nc.vector.scalar_tensor_tensor(
            out=neg_bias_temp[:], in0=bias_bf[:], scalar=-1.0, in1=temp_bf[:], op0=ALU.mult, op1=ALU.mult
        )

        neg_max = consts.tile([P, STATS], F32)
        row_sum = consts.tile([P, STATS], F32)
        inv_sum = consts.tile([P, STATS], F32)
        sum_pow = consts.tile([P, STATS], F32)
        exp_part = consts.tile([P, STATS], F32)

        penalty_cols = []
        for b in range(B):
            penalty_col = per_batch.tile([P, ROW_TILES], BF16)
            nc.gpsimd.tensor_scalar(
                out=penalty_col[:].rearrange("p (n o) -> p n o", o=1),
                in0=k_rows[b][:].rearrange("p (n d) -> p n d", n=ROW_TILES)[:, :, 0:1],
                scalar1=0.0,
                scalar2=MASKED,
                op0=ALU.is_equal,
                op1=ALU.mult,
            )
            penalty_cols.append(penalty_col)

        def transpose_words(rows, bank):
            words = rows[:].bitcast(F32)
            for piece in range(ROW_TILES * HALVES):
                cols = slice(piece * P, (piece + 1) * P)
                nc.tensor.transpose(out=bank[:, cols], in_=words[:, cols], identity=ident[:])

        operands = {}
        exps = {}

        def prepare(b, copy_keys):
            k_bank = psum.tile([P, BANK], F32)
            transpose_words(k_rows[b], k_bank)
            q_bank = psum.tile([P, BANK], F32)
            transpose_words(q_rows[b], q_bank)
            penalty_bank = psum.tile([P, BANK], F32)
            nc.tensor.transpose(
                out=penalty_bank[:, 0:P],
                in_=penalty_cols[b][:].bitcast(F32).to_broadcast([P, P]),
                identity=ident[:],
            )

            k_grouped = per_batch.tile([P, K * PACK], BF16, align_bytes=64)
            copy_keys(
                out=k_grouped[:].bitcast(F32).rearrange("w (p n h) -> w p n h", n=ROW_TILES, h=HALVES),
                in_=k_bank[:].rearrange("w (n h p) -> w p n h", n=ROW_TILES, h=HALVES),
            )
            q_grouped = per_batch.tile([P, Q * PACK], BF16, align_bytes=64)
            nc.scalar.copy(
                out=q_grouped[:].bitcast(F32).rearrange("w (n p h) -> w n p h", n=ROW_TILES, h=HALVES),
                in_=q_bank[:].rearrange("w (n h p) -> w n p h", n=ROW_TILES, h=HALVES),
            )
            penalty = per_batch.tile([P, K], BF16)
            nc.scalar.copy(out=penalty[:].bitcast(F32), in_=penalty_bank[:, 0:P])

            k_codes = per_batch.tile([P, K], U32, align_bytes=64)
            k_scales = per_batch.tile([P, K], U8, align_bytes=64)
            nc.vector.quantize_mx(out=k_codes[:].bitcast(FP8X4), scales=k_scales[:], in_=k_grouped[:])
            q_codes = per_batch.tile([P, Q], U32, align_bytes=64)
            q_scales = per_batch.tile([P, Q], U8, align_bytes=64)
            nc.vector.quantize_mx(out=q_codes[:].bitcast(FP8X4), scales=q_scales[:], in_=q_grouped[:])
            operands[b] = (k_codes, k_scales, q_codes, q_scales, penalty)

        def masked_logits(b):
            k_codes, k_scales, q_codes, q_scales, penalty = operands[b]
            logits = psum.tile([P, ROW_TILES * K], F32)
            for n in range(ROW_TILES):
                q_cols = slice(n * P, (n + 1) * P)
                nc.tensor.matmul_mx(
                    out=logits[:, n * K : (n + 1) * K],
                    lhsT=q_codes[:, q_cols].bitcast(FP8X4),
                    lhsT_scale=q_scales[:, q_cols],
                    rhs=k_codes[:].bitcast(FP8X4),
                    rhs_scale=k_scales[:],
                    start=True,
                    stop=True,
                )
            masked = per_batch.tile([P, ROW_TILES, K], F32)
            nc.vector.tensor_tensor(
                out=masked[:],
                in0=logits[:].rearrange("p (n k) -> p n k", n=ROW_TILES),
                in1=penalty[:].unsqueeze(1).to_broadcast([P, ROW_TILES, K]),
                op=ALU.add,
            )
            for n in range(ROW_TILES):
                col = b * ROW_TILES + n
                nc.vector.tensor_reduce(
                    out=neg_max[:, col : col + 1], in_=masked[:, n, :], axis=AXIS.X, op=ALU.max, negate=True
                )
            return masked

        def exponentials(b, masked):
            expd = per_batch.tile([P, ROW_TILES, K], F32)
            for n in range(ROW_TILES):
                col = b * ROW_TILES + n
                nc.scalar.activation(
                    out=expd[:, n, :],
                    in_=masked[:, n, :],
                    func=ACT.Exp,
                    bias=neg_max[:, col : col + 1],
                    accum_out=row_sum[:, col : col + 1],
                )
            stat_cols = slice(b * ROW_TILES, (b + 1) * ROW_TILES)
            nc.gpsimd.tensor_tensor(
                out=sum_pow[:, stat_cols],
                in0=row_sum[:, stat_cols],
                in1=neg_temp[:].to_broadcast([P, ROW_TILES]),
                op=ALU.pow,
            )
            nc.scalar.activation(
                out=exp_part[:, stat_cols],
                in_=neg_max[:, stat_cols],
                func=ACT.Exp,
                scale=temp[:],
                bias=neg_bias_temp[:],
            )
            exps[b] = expd

        def normalise(b):
            expd = exps[b]
            first = b * ROW_TILES
            stat_cols = slice(first, first + ROW_TILES)
            nc.vector.reciprocal(out=inv_sum[:, stat_cols], in_=row_sum[:, stat_cols])
            attn = per_batch.tile([P, ROW_TILES, K], F32)
            for n in range(ROW_TILES):
                nc.scalar.activation(
                    out=attn[:, n, :],
                    in_=expd[:, n, :],
                    func=ACT.Copy,
                    scale=inv_sum[:, first + n : first + n + 1],
                )
                nc.sync.dma_start(out=out_0[b, n * P : (n + 1) * P, :], in_=attn[:, n, :])

        for b in range(AHEAD):
            prepare(b, nc.vector.tensor_copy)
        for b in range(B):
            masked = masked_logits(b)
            if b + AHEAD < B:
                prepare(b + AHEAD, nc.scalar.copy)
            exponentials(b, masked)
            if b >= 1:
                normalise(b - 1)
        normalise(B - 1)

        denom = consts.tile([P, STATS], F32)
        nc.vector.tensor_tensor(out=denom[:], in0=sum_pow[:], in1=exp_part[:], op=ALU.mult)
        nc.vector.tensor_scalar_add(out=denom[:], in0=denom[:], scalar1=1.0)
        nc.vector.reciprocal(out=conf_cols[:, 0:STATS], in_=denom[:])
        conf_bank = psum.tile([P, BANK], F32, tag="penalty_bank")
        nc.tensor.transpose(out=conf_bank[:, 0:P], in_=conf_cols[:], identity=ident[:])
        conf_rows = consts.tile([P, P], F32)
        nc.vector.tensor_copy(out=conf_rows[:], in_=conf_bank[:, 0:P])
        nc.sync.dma_start(out=out_1.rearrange("b (n p) -> (b n) p", p=P), in_=conf_rows[0:STATS, :])
